import numpy as np
import ml_dtypes


def mxq(x, axis, fmt="e4m3"):
    dtype, down = {"e4m3": (ml_dtypes.float8_e4m3fn, 7), "e5m2": (ml_dtypes.float8_e5m2, 14)}[fmt]
    v = np.moveaxis(np.asarray(x, np.float32).astype(ml_dtypes.bfloat16).astype(np.float64), axis, -1)
    blocks = v.reshape(v.shape[:-1] + (-1, 32))
    amax = np.abs(blocks).max(-1, keepdims=True)
    byte = np.maximum(np.where(amax > 0, np.frexp(amax)[1] - 1 + 127, 0) - down, 1)
    scale = np.exp2(byte - 127.0)
    codes = (blocks / scale).astype(np.float32).astype(dtype).astype(np.float64)
    return np.moveaxis((codes * scale).reshape(v.shape), -1, axis)


WIDE = False


def mx_kscale(k):
    if not WIDE:
        return np.ones(k)
    levels = np.array([10, -10, 5, -5, 0])
    a = np.random.permutation(np.resize(levels, k // 512 * 4)).reshape(k // 512, 4)
    idx = np.arange(k)
    return np.exp2(a[idx // 512, idx % 128 // 32])


BF16 = ml_dtypes.bfloat16


def bf(x):
    return np.asarray(x, np.float32).astype(BF16)


def f64(x):
    return np.asarray(x).astype(np.float64)


B_, S, D_IN, D_OUT, N, RANK, ALPHA = 4, 2048, 512, 256, 32, 16, 32
NR = N * RANK
SCALE = ALPHA / RANK


def setup_inputs():
    s, t = mx_kscale(D_IN), mx_kscale(NR)
    tn = t.reshape(N, RANK)
    return {"x": bf(np.random.standard_normal((B_, S, D_IN)) * s),
            "lora_A": bf(np.random.standard_normal((N, RANK, D_IN)) / np.sqrt(D_IN) / s * tn[:, :, None]),
            "lora_B": bf(np.random.standard_normal((N, D_OUT, RANK)) / np.sqrt(RANK) / tn[:, None, :]),
            "W": bf(np.random.standard_normal((D_OUT, D_IN)) / np.sqrt(D_IN) / s),
            "bias": bf(np.random.standard_normal(D_OUT) * 0.3),
            "lora_weights": bf((1.0 + 0.5 * np.random.standard_normal(N)) * 2.0 / N)}


def reference(x, lora_A, lora_B, W, bias, lora_weights):
    xq = mxq(f64(x), 2, "e4m3")
    h = xq @ mxq(f64(lora_A).reshape(NR, D_IN), 1, "e4m3").T
    coef = (SCALE * f64(lora_weights))[:, None, None]
    bc = (f64(lora_B) * coef).transpose(1, 0, 2).reshape(D_OUT, NR)
    lora_out = mxq(h, 2, "e4m3") @ mxq(bc, 1, "e4m3").T
    base = (xq @ mxq(f64(W), 1, "e4m3").T) + f64(bias)
    return base + lora_out

@@ -1,0 +1,200 @@
+from contextlib import ExitStack
+
+import concourse.mybir as mybir
+from concourse.masks import make_identity
+
+F32 = mybir.dt.float32
+BF16 = mybir.dt.bfloat16
+U32 = mybir.dt.uint32
+U8 = mybir.dt.uint8
+FP8X4 = mybir.dt.float8_e4m3fn_x4
+
+P = 128
+PACK = 4
+K = P * PACK
+HALVES = 2
+SUBS = 4
+TILE = SUBS * P
+LORA_SCALE = 2.0
+OUT_LAG = 2
+
+FLOPS = 2 * 8192 * 512 * (512 + 256 + 256)
+
+
+def tile_replaced_compose_lora_pa_t_kernel(tc, x, lora_A, lora_B, W, bias, lora_weights, out):
+    nc = tc.nc
+    x_rows = x.flatten_outer_dims()
+    out_rows = out.flatten_outer_dims()
+    a_rows = lora_A.flatten_outer_dims()
+    rank = lora_A.shape[1]
+    d_out = W.shape[0]
+    n_tiles = x_rows.shape[0] // TILE
+    assert x_rows.shape[1] == K and a_rows.shape[0] == K and d_out == 2 * P
+
+    with ExitStack() as ctx:
+        fixed = ctx.enter_context(tc.tile_pool(name="fixed", bufs=1))
+        x_pool = ctx.enter_context(tc.tile_pool(name="x_pool", bufs=n_tiles))
+        grouped_pool = ctx.enter_context(tc.tile_pool(name="grouped_pool", bufs=2))
+        codes_pool = ctx.enter_context(tc.tile_pool(name="codes_pool", bufs=OUT_LAG + 2))
+        result_pool = ctx.enter_context(tc.tile_pool(name="result_pool", bufs=3))
+        psum_t = ctx.enter_context(tc.psum_pool(name="psum_t", bufs=2))
+        psum_h = ctx.enter_context(tc.psum_pool(name="psum_h", bufs=4))
+        psum_o = ctx.enter_context(tc.psum_pool(name="psum_o", bufs=2))
+        ctx.enter_context(tc.manual_schedule())
+
+        def load_x(i):
+            x_tile = x_pool.tile([P, SUBS, K], BF16, name="x_tile")
+            nc.sync.dma_start(
+                out=x_tile[:],
+                in_=x_rows[i * TILE : (i + 1) * TILE, :].rearrange("(c s) d -> c s d", s=SUBS),
+            )
+            return x_tile
+
+        a_in = fixed.tile([P, PACK, K], BF16)
+        nc.sync.dma_start(out=a_in[:], in_=a_rows.rearrange("(c t) d -> c t d", t=PACK))
+        x_in = [load_x(i) for i in range(OUT_LAG + 1)]
+        w_in = fixed.tile([P, 2, K], BF16)
+        nc.sync.dma_start(out=w_in[:], in_=W.rearrange("(s c) d -> c s d", c=P))
+        b_in = fixed.tile([P, 2, K], BF16)
+        for half in range(2):
+            nc.sync.dma_start(
+                out=b_in[:, half, :].rearrange("o (n r) -> o n r", r=rank),
+                in_=lora_B[:, half * P : (half + 1) * P, :].rearrange("n o r -> o n r"),
+            )
+        x_in.extend([load_x(i) for i in range(OUT_LAG + 1, n_tiles)])
+
+        mix_bf = fixed.tile([P, 1], BF16)
+        for a in range(PACK):
+            nc.scalar.dma_start(out=mix_bf[a:P:PACK, :], in_=lora_weights.rearrange("(n one) -> n one", one=1))
+        bias_bf = fixed.tile([P, d_out], BF16)
+        nc.scalar.dma_start(out=bias_bf[:], in_=bias.partition_broadcast(P))
+
+        ident = fixed.tile([P, P], F32)
+        make_identity(nc, ident[:])
+
+        def quantise(grouped, pool, label):
+            columns = grouped.shape[1]
+            codes = pool.tile([P, columns], U32, name=label + "_codes", align_bytes=64)
+            scales = pool.tile([P, columns], U8, name=label + "_scales", align_bytes=64)
+            nc.vector.quantize_mx(
+                out=codes[:].bitcast(FP8X4),
+                scales=scales[:],
+                in_=grouped[:].rearrange("p c t -> p (c t)"),
+            )
+            return codes, scales
+
+        def quantise_rows(rows, psum, bank_tag, grouped_from, codes_from, label):
+            subs = rows.shape[1]
+            grouped = grouped_from.tile([P, subs * P, PACK], BF16, name=label + "_grouped", align_bytes=64)
+            grouped_words = grouped[:].bitcast(F32)
+            for pair in range(subs // 2):
+                bank = psum.tile([P, HALVES, 2, P], F32, name=label + "_bank", tag=bank_tag)
+                for s in range(2):
+                    words = rows[:, 2 * pair + s, :].bitcast(F32)
+                    for u in range(HALVES):
+                        nc.tensor.transpose(out=bank[:, u, s, :], in_=words[:, u * P : (u + 1) * P], identity=ident[:])
+                leave = nc.scalar.copy if pair % 2 == 0 else nc.vector.tensor_copy
+                leave(
+                    out=grouped_words[:, 2 * pair * P : 2 * (pair + 1) * P, :],
+                    in_=bank[:].rearrange("p u s c -> p (s c) u"),
+                )
+            return quantise(grouped, codes_from, label)
+
+        def prepare_out_weights():
+            w_mx = quantise_rows(w_in, psum_o, "out_bank", fixed, fixed, "w")
+
+            mix = fixed.tile([P, 1], F32)
+            nc.vector.tensor_scalar(
+                out=mix[:], in0=mix_bf[:], scalar1=LORA_SCALE, scalar2=None, op0=mybir.AluOpType.mult
+            )
+            bank = psum_o.tile([P, HALVES, 2, P], F32, name="b_bank", tag="out_bank")
+            for half in range(2):
+                words = b_in[:, half, :].bitcast(F32).rearrange("o (q u) -> o u q", u=HALVES)
+                for u in range(HALVES):
+                    nc.tensor.transpose(out=bank[:, u, half, :], in_=words[:, u, :], identity=ident[:])
+            b_grouped = fixed.tile([P, d_out, PACK], BF16, align_bytes=64)
+            nc.vector.tensor_scalar(
+                out=b_grouped[:].rearrange("q o (u e) -> q o u e", u=HALVES),
+                in0=bank[:].bitcast(BF16).rearrange("q u h (c e) -> q (h c) u e", e=2),
+                scalar1=mix[:, 0:1],
+                scalar2=None,
+                op0=mybir.AluOpType.mult,
+            )
+            b_mx = quantise(b_grouped, fixed, "b")
+
+            bias_twice = fixed.tile([P, 2, d_out], F32)
+            nc.vector.tensor_copy(out=bias_twice[:], in_=bias_bf[:].unsqueeze(1).to_broadcast([P, 2, d_out]))
+            return w_mx, b_mx, bias_twice
+
+        x_mx = {}
+        h_grouped = {}
+        h_mx = {}
+
+        def low_rank_passes(i):
+            x_codes, x_scales = x_mx[i]
+            h_grouped[i] = grouped_pool.tile([P, TILE, PACK], BF16, name="h_grouped", align_bytes=64)
+            for s in range(SUBS):
+                tokens = slice(s * P, (s + 1) * P)
+                bank = psum_h.tile([P, PACK, P], F32, name="h_bank", tag="h_bank")
+                for t in range(PACK):
+                    ks = slice(t * P, (t + 1) * P)
+                    nc.tensor.matmul_mx(
+                        out=bank[:, t, :],
+                        lhsT=a_codes[:, ks].bitcast(FP8X4),
+                        lhsT_scale=a_scales[:, ks],
+                        rhs=x_codes[:, tokens].bitcast(FP8X4),
+                        rhs_scale=x_scales[:, tokens],
+                        start=True,
+                        stop=True,
+                    )
+                nc.scalar.copy(out=h_grouped[i][:, tokens, :], in_=bank[:].rearrange("p t c -> p c t"))
+
+        def out_passes(i):
+            x_codes, x_scales = x_mx[i]
+            h_codes, h_scales = h_mx[i]
+            result = result_pool.tile([P, SUBS, d_out], F32, name="result")
+            for pair in range(SUBS // 2):
+                bank = psum_o.tile([P, 2, d_out], F32, name="out_bank", tag="out_bank")
+                for j in range(2):
+                    tokens = slice((2 * pair + j) * P, (2 * pair + j + 1) * P)
+                    nc.tensor.matmul_mx(
+                        out=bank[:, j, :],
+                        lhsT=x_codes[:, tokens].bitcast(FP8X4),
+                        lhsT_scale=x_scales[:, tokens],
+                        rhs=w_codes[:].bitcast(FP8X4),
+                        rhs_scale=w_scales[:],
+                        start=True,
+                        stop=False,
+                    )
+                    nc.tensor.matmul_mx(
+                        out=bank[:, j, :],
+                        lhsT=h_codes[:, tokens].bitcast(FP8X4),
+                        lhsT_scale=h_scales[:, tokens],
+                        rhs=b_codes[:].bitcast(FP8X4),
+                        rhs_scale=b_scales[:],
+                        start=False,
+                        stop=True,
+                    )
+                nc.vector.tensor_tensor(
+                    out=result[:, 2 * pair : 2 * pair + 2, :], in0=bank[:], in1=bias_twice[:], op=mybir.AluOpType.add
+                )
+            nc.sync.dma_start(
+                out=out_rows[i * TILE : (i + 1) * TILE, :].rearrange("(c s) o -> c s o", s=SUBS), in_=result[:]
+            )
+
+        def step(j):
+            if 0 <= j - OUT_LAG < n_tiles:
+                out_passes(j - OUT_LAG)
+            if 0 <= j - 1 < n_tiles:
+                h_mx[j - 1] = quantise(h_grouped[j - 1], codes_pool, "h")
+            if 0 <= j + 1 < n_tiles:
+                x_mx[j + 1] = quantise_rows(x_in[j + 1], psum_t, "x_bank", grouped_pool, codes_pool, "x")
+            if 0 <= j < n_tiles:
+                low_rank_passes(j)
+
+        a_codes, a_scales = quantise_rows(a_in, psum_h, "h_bank", fixed, fixed, "a")
+        for j in range(-1, OUT_LAG):
+            step(j)
+        (w_codes, w_scales), (b_codes, b_scales), bias_twice = prepare_out_weights()
+        for j in range(OUT_LAG, n_tiles + OUT_LAG):
+            step(j)

@@ -16,6 +16,7 @@ HALVES = 2
 SUBS = 4
 TILE = SUBS * P
 LORA_SCALE = 2.0
+QUARTER = 64
 OUT_LAG = 2
 
 FLOPS = 2 * 8192 * 512 * (512 + 256 + 256)
@@ -35,7 +36,7 @@ def tile_replaced_compose_lora_pa_t_kernel(tc, x, lora_A, lora_B, W, bias, lora_
         fixed = ctx.enter_context(tc.tile_pool(name="fixed", bufs=1))
         x_pool = ctx.enter_context(tc.tile_pool(name="x_pool", bufs=n_tiles))
         grouped_pool = ctx.enter_context(tc.tile_pool(name="grouped_pool", bufs=2))
-        codes_pool = ctx.enter_context(tc.tile_pool(name="codes_pool", bufs=OUT_LAG + 2))
+        codes_pool = ctx.enter_context(tc.tile_pool(name="codes_pool", bufs=OUT_LAG + 3))
         result_pool = ctx.enter_context(tc.tile_pool(name="result_pool", bufs=3))
         psum_t = ctx.enter_context(tc.psum_pool(name="psum_t", bufs=2))
         psum_h = ctx.enter_context(tc.psum_pool(name="psum_h", bufs=4))
@@ -52,22 +53,19 @@ def tile_replaced_compose_lora_pa_t_kernel(tc, x, lora_A, lora_B, W, bias, lora_
 
         a_in = fixed.tile([P, PACK, K], BF16)
         nc.sync.dma_start(out=a_in[:], in_=a_rows.rearrange("(c t) d -> c t d", t=PACK))
-        x_in = [load_x(i) for i in range(OUT_LAG + 1)]
+        x_in = [load_x(i) for i in range(2)]
+        b_in = fixed.tile([P, QUARTER * rank], BF16)
+        nc.sync.dma_start(out=b_in[:], in_=lora_B.rearrange("n (oh ol) r -> (n oh) (ol r)", ol=QUARTER))
         w_in = fixed.tile([P, 2, K], BF16)
         nc.sync.dma_start(out=w_in[:], in_=W.rearrange("(s c) d -> c s d", c=P))
-        b_in = fixed.tile([P, 2, K], BF16)
-        for half in range(2):
-            nc.sync.dma_start(
-                out=b_in[:, half, :].rearrange("o (n r) -> o n r", r=rank),
-                in_=lora_B[:, half * P : (half + 1) * P, :].rearrange("n o r -> o n r"),
-            )
-        x_in.extend([load_x(i) for i in range(OUT_LAG + 1, n_tiles)])
+        x_in.extend([load_x(i) for i in range(2, n_tiles)])
 
-        mix_bf = fixed.tile([P, 1], BF16)
+        mix = fixed.tile([P, 1], BF16)
         for a in range(PACK):
-            nc.scalar.dma_start(out=mix_bf[a:P:PACK, :], in_=lora_weights.rearrange("(n one) -> n one", one=1))
-        bias_bf = fixed.tile([P, d_out], BF16)
-        nc.scalar.dma_start(out=bias_bf[:], in_=bias.partition_broadcast(P))
+            nc.scalar.dma_start(out=mix[a:P:PACK, :], in_=lora_weights.rearrange("(n one) -> n one", one=1))
+        bias_all = fixed.tile([P, d_out], BF16)
+        nc.scalar.dma_start(out=bias_all[:], in_=bias.partition_broadcast(P))
+        bias_twice = bias_all[:].unsqueeze(1).to_broadcast([P, 2, d_out])
 
         ident = fixed.tile([P, P], F32)
         make_identity(nc, ident[:])
@@ -93,38 +91,46 @@ def tile_replaced_compose_lora_pa_t_kernel(tc, x, lora_A, lora_B, W, bias, lora_
                     words = rows[:, 2 * pair + s, :].bitcast(F32)
                     for u in range(HALVES):
                         nc.tensor.transpose(out=bank[:, u, s, :], in_=words[:, u * P : (u + 1) * P], identity=ident[:])
-                leave = nc.scalar.copy if pair % 2 == 0 else nc.vector.tensor_copy
+                leave = nc.vector.tensor_copy if pair == subs // 2 - 1 else nc.scalar.copy
                 leave(
                     out=grouped_words[:, 2 * pair * P : 2 * (pair + 1) * P, :],
                     in_=bank[:].rearrange("p u s c -> p (s c) u"),
                 )
             return quantise(grouped, codes_from, label)
 
-        def prepare_out_weights():
-            w_mx = quantise_rows(w_in, psum_o, "out_bank", fixed, fixed, "w")
-
-            mix = fixed.tile([P, 1], F32)
-            nc.vector.tensor_scalar(
-                out=mix[:], in0=mix_bf[:], scalar1=LORA_SCALE, scalar2=None, op0=mybir.AluOpType.mult
+        def sort_b():
+            b_sorted = fixed.tile([P, PACK, P], F32)
+            nc.scalar.copy(
+                out=b_sorted[:].rearrange("q a (ol w) -> q a ol w", w=2),
+                in_=b_in[:].bitcast(F32).rearrange("q (ol a w) -> q a ol w", a=PACK, w=2),
             )
-            bank = psum_o.tile([P, HALVES, 2, P], F32, name="b_bank", tag="out_bank")
-            for half in range(2):
-                words = b_in[:, half, :].bitcast(F32).rearrange("o (q u) -> o u q", u=HALVES)
-                for u in range(HALVES):
-                    nc.tensor.transpose(out=bank[:, u, half, :], in_=words[:, u, :], identity=ident[:])
+            return b_sorted
+
+        def turn_b_first(b_sorted):
+            bank = psum_o.tile([P, PACK, P], F32, name="b_bank_first", tag="out_bank")
+            for a in range(PACK):
+                nc.tensor.transpose(out=bank[:, a, :], in_=b_sorted[:, a, :], identity=ident[:])
+            b_turned = fixed.tile([P, PACK, P], F32)
+            nc.vector.tensor_copy(
+                out=b_turned[:].rearrange("v oh (n a) -> v oh n a", a=PACK),
+                in_=bank[:].rearrange("v a (n oh) -> v oh n a", oh=PACK),
+            )
+            return b_turned
+
+        def turn_b_second(b_turned):
+            bank = psum_o.tile([P, PACK, P], F32, name="b_bank_second", tag="out_bank")
+            for oh in range(PACK):
+                nc.tensor.transpose(out=bank[:, oh, :], in_=b_turned[:, oh, :], identity=ident[:])
             b_grouped = fixed.tile([P, d_out, PACK], BF16, align_bytes=64)
             nc.vector.tensor_scalar(
-                out=b_grouped[:].rearrange("q o (u e) -> q o u e", u=HALVES),
-                in0=bank[:].bitcast(BF16).rearrange("q u h (c e) -> q (h c) u e", e=2),
+                out=b_grouped[:].rearrange("q o t -> q (o t)"),
+                in0=bank[:].bitcast(BF16).rearrange("q oh v -> q (oh v)"),
                 scalar1=mix[:, 0:1],
-                scalar2=None,
+                scalar2=LORA_SCALE,
                 op0=mybir.AluOpType.mult,
+                op1=mybir.AluOpType.mult,
             )
-            b_mx = quantise(b_grouped, fixed, "b")
-
-            bias_twice = fixed.tile([P, 2, d_out], F32)
-            nc.vector.tensor_copy(out=bias_twice[:], in_=bias_bf[:].unsqueeze(1).to_broadcast([P, 2, d_out]))
-            return w_mx, b_mx, bias_twice
+            return quantise(b_grouped, fixed, "b")
 
         x_mx = {}
         h_grouped = {}
@@ -176,25 +182,30 @@ def tile_replaced_compose_lora_pa_t_kernel(tc, x, lora_A, lora_B, W, bias, lora_
                         stop=True,
                     )
                 nc.vector.tensor_tensor(
-                    out=result[:, 2 * pair : 2 * pair + 2, :], in0=bank[:], in1=bias_twice[:], op=mybir.AluOpType.add
+                    out=result[:, 2 * pair : 2 * pair + 2, :], in0=bank[:], in1=bias_twice, op=mybir.AluOpType.add
                 )
             nc.sync.dma_start(
                 out=out_rows[i * TILE : (i + 1) * TILE, :].rearrange("(c s) o -> c s o", s=SUBS), in_=result[:]
             )
 
         def step(j):
-            if 0 <= j - OUT_LAG < n_tiles:
-                out_passes(j - OUT_LAG)
-            if 0 <= j - 1 < n_tiles:
-                h_mx[j - 1] = quantise(h_grouped[j - 1], codes_pool, "h")
-            if 0 <= j + 1 < n_tiles:
-                x_mx[j + 1] = quantise_rows(x_in[j + 1], psum_t, "x_bank", grouped_pool, codes_pool, "x")
-            if 0 <= j < n_tiles:
+            if j < n_tiles:
                 low_rank_passes(j)
+            if 0 <= j - OUT_LAG:
+                out_passes(j - OUT_LAG)
+            if j < n_tiles:
+                h_mx[j] = quantise(h_grouped[j], codes_pool, "h")
+            if j + 2 < n_tiles:
+                x_mx[j + 2] = quantise_rows(x_in[j + 2], psum_t, "x_bank", grouped_pool, codes_pool, "x")
 
         a_codes, a_scales = quantise_rows(a_in, psum_h, "h_bank", fixed, fixed, "a")
-        for j in range(-1, OUT_LAG):
-            step(j)
-        (w_codes, w_scales), (b_codes, b_scales), bias_twice = prepare_out_weights()
-        for j in range(OUT_LAG, n_tiles + OUT_LAG):
+        for i in range(2):
+            x_mx[i] = quantise_rows(x_in[i], psum_t, "x_bank", grouped_pool, codes_pool, "x")
+        b_sorted = sort_b()
+        step(0)
+        b_turned = turn_b_first(b_sorted)
+        w_codes, w_scales = quantise_rows(w_in, psum_o, "out_bank", fixed, fixed, "w")
+        step(1)
+        b_codes, b_scales = turn_b_second(b_turned)
+        for j in range(2, n_tiles + OUT_LAG):
             step(j)

@@ -81,7 +81,7 @@ def tile_replaced_compose_lora_pa_t_kernel(tc, x, lora_A, lora_B, W, bias, lora_
             )
             return codes, scales
 
-        def quantise_rows(rows, psum, bank_tag, grouped_from, codes_from, label):
+        def turn_rows(rows, psum, bank_tag, grouped_from, label, leave_last_bank):
             subs = rows.shape[1]
             grouped = grouped_from.tile([P, subs * P, PACK], BF16, name=label + "_grouped", align_bytes=64)
             grouped_words = grouped[:].bitcast(F32)
@@ -91,12 +91,12 @@ def tile_replaced_compose_lora_pa_t_kernel(tc, x, lora_A, lora_B, W, bias, lora_
                     words = rows[:, 2 * pair + s, :].bitcast(F32)
                     for u in range(HALVES):
                         nc.tensor.transpose(out=bank[:, u, s, :], in_=words[:, u * P : (u + 1) * P], identity=ident[:])
-                leave = nc.vector.tensor_copy if pair == subs // 2 - 1 else nc.scalar.copy
+                leave = leave_last_bank if pair == subs // 2 - 1 else nc.scalar.copy
                 leave(
                     out=grouped_words[:, 2 * pair * P : 2 * (pair + 1) * P, :],
                     in_=bank[:].rearrange("p u s c -> p (s c) u"),
                 )
-            return quantise(grouped, codes_from, label)
+            return grouped
 
         def sort_b():
             b_sorted = fixed.tile([P, PACK, P], F32)
@@ -188,23 +188,29 @@ def tile_replaced_compose_lora_pa_t_kernel(tc, x, lora_A, lora_B, W, bias, lora_
                 out=out_rows[i * TILE : (i + 1) * TILE, :].rearrange("(c s) o -> c s o", s=SUBS), in_=result[:]
             )
 
+        def turn_x(i):
+            leave_last_bank = nc.vector.tensor_copy if i < OUT_LAG + 2 else nc.scalar.copy
+            return turn_rows(x_in[i], psum_t, "x_bank", grouped_pool, "x", leave_last_bank)
+
         def step(j):
             if j < n_tiles:
                 low_rank_passes(j)
-            if 0 <= j - OUT_LAG:
-                out_passes(j - OUT_LAG)
+            if j + 2 < n_tiles:
+                x_grouped = turn_x(j + 2)
             if j < n_tiles:
                 h_mx[j] = quantise(h_grouped[j], codes_pool, "h")
+            if 0 <= j - OUT_LAG:
+                out_passes(j - OUT_LAG)
             if j + 2 < n_tiles:
-                x_mx[j + 2] = quantise_rows(x_in[j + 2], psum_t, "x_bank", grouped_pool, codes_pool, "x")
+                x_mx[j + 2] = quantise(x_grouped, codes_pool, "x")
 
-        a_codes, a_scales = quantise_rows(a_in, psum_h, "h_bank", fixed, fixed, "a")
+        a_codes, a_scales = quantise(turn_rows(a_in, psum_h, "h_bank", fixed, "a", nc.vector.tensor_copy), fixed, "a")
         for i in range(2):
-            x_mx[i] = quantise_rows(x_in[i], psum_t, "x_bank", grouped_pool, codes_pool, "x")
+            x_mx[i] = quantise(turn_x(i), codes_pool, "x")
         b_sorted = sort_b()
         step(0)
         b_turned = turn_b_first(b_sorted)
-        w_codes, w_scales = quantise_rows(w_in, psum_o, "out_bank", fixed, fixed, "w")
+        w_codes, w_scales = quantise(turn_rows(w_in, psum_o, "out_bank", fixed, "w", nc.vector.tensor_copy), fixed, "w")
         step(1)
         b_codes, b_scales = turn_b_second(b_turned)
         for j in range(2, n_tiles + OUT_LAG):

@@ -37,7 +37,7 @@ def tile_replaced_compose_lora_pa_t_kernel(tc, x, lora_A, lora_B, W, bias, lora_
         x_pool = ctx.enter_context(tc.tile_pool(name="x_pool", bufs=n_tiles))
         grouped_pool = ctx.enter_context(tc.tile_pool(name="grouped_pool", bufs=2))
         codes_pool = ctx.enter_context(tc.tile_pool(name="codes_pool", bufs=OUT_LAG + 3))
-        result_pool = ctx.enter_context(tc.tile_pool(name="result_pool", bufs=3))
+        result_pool = ctx.enter_context(tc.tile_pool(name="result_pool", bufs=4))
         psum_t = ctx.enter_context(tc.psum_pool(name="psum_t", bufs=2))
         psum_h = ctx.enter_context(tc.psum_pool(name="psum_h", bufs=4))
         psum_o = ctx.enter_context(tc.psum_pool(name="psum_o", bufs=2))
@@ -70,23 +70,14 @@ def tile_replaced_compose_lora_pa_t_kernel(tc, x, lora_A, lora_B, W, bias, lora_
         ident = fixed.tile([P, P], F32)
         make_identity(nc, ident[:])
 
-        def quantise(grouped, pool, label):
-            columns = grouped.shape[1]
-            codes = pool.tile([P, columns], U32, name=label + "_codes", align_bytes=64)
-            scales = pool.tile([P, columns], U8, name=label + "_scales", align_bytes=64)
-            nc.vector.quantize_mx(
-                out=codes[:].bitcast(FP8X4),
-                scales=scales[:],
-                in_=grouped[:].rearrange("p c t -> p (c t)"),
-            )
-            return codes, scales
+        def quantise(grouped, codes, scales):
+            nc.vector.quantize_mx(out=codes.bitcast(FP8X4), scales=scales, in_=grouped)
 
-        def turn_rows(rows, psum, bank_tag, grouped_from, label, leave_last_bank):
+        def turn_rows(rows, grouped, psum, bank_tag, leave_last_bank):
             subs = rows.shape[1]
-            grouped = grouped_from.tile([P, subs * P, PACK], BF16, name=label + "_grouped", align_bytes=64)
-            grouped_words = grouped[:].bitcast(F32)
+            grouped_words = grouped.bitcast(F32)
             for pair in range(subs // 2):
-                bank = psum.tile([P, HALVES, 2, P], F32, name=label + "_bank", tag=bank_tag)
+                bank = psum.tile([P, HALVES, 2, P], F32, name="turn_bank", tag=bank_tag)
                 for s in range(2):
                     words = rows[:, 2 * pair + s, :].bitcast(F32)
                     for u in range(HALVES):
@@ -96,7 +87,15 @@ def tile_replaced_compose_lora_pa_t_kernel(tc, x, lora_A, lora_B, W, bias, lora_
                     out=grouped_words[:, 2 * pair * P : 2 * (pair + 1) * P, :],
                     in_=bank[:].rearrange("p u s c -> p (s c) u"),
                 )
-            return grouped
+
+        def weight_words(rows, psum, bank_tag, label):
+            columns = rows.shape[1] * P
+            grouped = fixed.tile([P, columns, PACK], BF16, name=label + "_grouped", align_bytes=64)
+            codes = fixed.tile([P, columns], U32, name=label + "_codes", align_bytes=64)
+            scales = fixed.tile([P, columns], U8, name=label + "_scales", align_bytes=64)
+            turn_rows(rows, grouped[:], psum, bank_tag, nc.vector.tensor_copy)
+            quantise(grouped[:].rearrange("p c t -> p (c t)"), codes[:], scales[:])
+            return codes, scales
 
         def sort_b():
             b_sorted = fixed.tile([P, PACK, P], F32)
@@ -121,24 +120,25 @@ def tile_replaced_compose_lora_pa_t_kernel(tc, x, lora_A, lora_B, W, bias, lora_
             bank = psum_o.tile([P, PACK, P], F32, name="b_bank_second", tag="out_bank")
             for oh in range(PACK):
                 nc.tensor.transpose(out=bank[:, oh, :], in_=b_turned[:, oh, :], identity=ident[:])
-            b_grouped = fixed.tile([P, d_out, PACK], BF16, align_bytes=64)
+            b_grouped = fixed.tile([P, d_out * PACK], BF16, align_bytes=64)
             nc.vector.tensor_scalar(
-                out=b_grouped[:].rearrange("q o t -> q (o t)"),
+                out=b_grouped[:],
                 in0=bank[:].bitcast(BF16).rearrange("q oh v -> q (oh v)"),
                 scalar1=mix[:, 0:1],
                 scalar2=LORA_SCALE,
                 op0=mybir.AluOpType.mult,
                 op1=mybir.AluOpType.mult,
             )
-            return quantise(b_grouped, fixed, "b")
+            codes = fixed.tile([P, d_out], U32, name="b_codes", align_bytes=64)
+            scales = fixed.tile([P, d_out], U8, name="b_scales", align_bytes=64)
+            quantise(b_grouped[:], codes[:], scales[:])
+            return codes, scales
 
         x_mx = {}
-        h_grouped = {}
         h_mx = {}
 
-        def low_rank_passes(i):
+        def low_rank_passes(i, h_grouped):
             x_codes, x_scales = x_mx[i]
-            h_grouped[i] = grouped_pool.tile([P, TILE, PACK], BF16, name="h_grouped", align_bytes=64)
             for s in range(SUBS):
                 tokens = slice(s * P, (s + 1) * P)
                 bank = psum_h.tile([P, PACK, P], F32, name="h_bank", tag="h_bank")
@@ -153,12 +153,12 @@ def tile_replaced_compose_lora_pa_t_kernel(tc, x, lora_A, lora_B, W, bias, lora_
                         start=True,
                         stop=True,
                     )
-                nc.scalar.copy(out=h_grouped[i][:, tokens, :], in_=bank[:].rearrange("p t c -> p c t"))
+                nc.scalar.copy(out=h_grouped[:, tokens, :], in_=bank[:].rearrange("p t c -> p c t"))
 
         def out_passes(i):
             x_codes, x_scales = x_mx[i]
             h_codes, h_scales = h_mx[i]
-            result = result_pool.tile([P, SUBS, d_out], F32, name="result")
+            out_tile = out_rows[i * TILE : (i + 1) * TILE, :].rearrange("(c s) o -> c s o", s=SUBS)
             for pair in range(SUBS // 2):
                 bank = psum_o.tile([P, 2, d_out], F32, name="out_bank", tag="out_bank")
                 for j in range(2):
@@ -181,36 +181,43 @@ def tile_replaced_compose_lora_pa_t_kernel(tc, x, lora_A, lora_B, W, bias, lora_
                         start=False,
                         stop=True,
                     )
-                nc.vector.tensor_tensor(
-                    out=result[:, 2 * pair : 2 * pair + 2, :], in0=bank[:], in1=bias_twice, op=mybir.AluOpType.add
-                )
-            nc.sync.dma_start(
-                out=out_rows[i * TILE : (i + 1) * TILE, :].rearrange("(c s) o -> c s o", s=SUBS), in_=result[:]
-            )
-
-        def turn_x(i):
-            leave_last_bank = nc.vector.tensor_copy if i < OUT_LAG + 2 else nc.scalar.copy
-            return turn_rows(x_in[i], psum_t, "x_bank", grouped_pool, "x", leave_last_bank)
+                result = result_pool.tile([P, 2, d_out], F32, name="result")
+                nc.vector.tensor_tensor(out=result[:], in0=bank[:], in1=bias_twice, op=mybir.AluOpType.add)
+                nc.sync.dma_start(out=out_tile[:, 2 * pair : 2 * pair + 2, :], in_=result[:])
 
         def step(j):
-            if j < n_tiles:
-                low_rank_passes(j)
-            if j + 2 < n_tiles:
-                x_grouped = turn_x(j + 2)
-            if j < n_tiles:
-                h_mx[j] = quantise(h_grouped[j], codes_pool, "h")
+            has_h = 0 <= j < n_tiles
+            has_x = 0 <= j + 2 < n_tiles
+            if has_h or has_x:
+                grouped = grouped_pool.tile([P, 2, TILE, PACK], BF16, name="grouped", align_bytes=64)
+                codes = codes_pool.tile([P, 2, TILE], U32, name="codes", align_bytes=64)
+                scales = codes_pool.tile([P, 2, TILE], U8, name="scales", align_bytes=64)
+            if has_h:
+                low_rank_passes(j, grouped[:, 0])
+                h_mx[j] = (codes[:, 0], scales[:, 0])
+            if has_x:
+                by_vector = j % 2 == 0 or j < OUT_LAG
+                turn_rows(
+                    x_in[j + 2], grouped[:, 1], psum_t, "x_bank", nc.vector.tensor_copy if by_vector else nc.scalar.copy
+                )
+                x_mx[j + 2] = (codes[:, 1], scales[:, 1])
             if 0 <= j - OUT_LAG:
                 out_passes(j - OUT_LAG)
-            if j + 2 < n_tiles:
-                x_mx[j + 2] = quantise(x_grouped, codes_pool, "x")
+            if has_h or has_x:
+                filled = slice(0 if has_h else 1, 2 if has_x else 1)
+                quantise(
+                    grouped[:, filled].rearrange("p g c t -> p (g c t)"),
+                    codes[:, filled].rearrange("p g c -> p (g c)"),
+                    scales[:, filled].rearrange("p g c -> p (g c)"),
+                )
 
-        a_codes, a_scales = quantise(turn_rows(a_in, psum_h, "h_bank", fixed, "a", nc.vector.tensor_copy), fixed, "a")
-        for i in range(2):
-            x_mx[i] = quantise(turn_x(i), codes_pool, "x")
+        a_codes, a_scales = weight_words(a_in, psum_h, "h_bank", "a")
+        step(-2)
+        step(-1)
         b_sorted = sort_b()
         step(0)
         b_turned = turn_b_first(b_sorted)
-        w_codes, w_scales = quantise(turn_rows(w_in, psum_o, "out_bank", fixed, "w", nc.vector.tensor_copy), fixed, "w")
+        w_codes, w_scales = weight_words(w_in, psum_o, "out_bank", "w")
         step(1)
         b_codes, b_scales = turn_b_second(b_turned)
         for j in range(2, n_tiles + OUT_LAG):

@@ -18,6 +18,7 @@ TILE = SUBS * P
 LORA_SCALE = 2.0
 QUARTER = 64
 OUT_LAG = 2
+X_RUN = 2
 
 FLOPS = 2 * 8192 * 512 * (512 + 256 + 256)
 
@@ -30,17 +31,15 @@ def tile_replaced_compose_lora_pa_t_kernel(tc, x, lora_A, lora_B, W, bias, lora_
     rank = lora_A.shape[1]
     d_out = W.shape[0]
     n_tiles = x_rows.shape[0] // TILE
-    assert x_rows.shape[1] == K and a_rows.shape[0] == K and d_out == 2 * P
+    assert x_rows.shape[1] == K and a_rows.shape[0] == K and d_out == 2 * P and n_tiles % X_RUN == 0
 
     with ExitStack() as ctx:
         fixed = ctx.enter_context(tc.tile_pool(name="fixed", bufs=1))
         x_pool = ctx.enter_context(tc.tile_pool(name="x_pool", bufs=n_tiles))
-        grouped_pool = ctx.enter_context(tc.tile_pool(name="grouped_pool", bufs=2))
+        grouped_pool = ctx.enter_context(tc.tile_pool(name="grouped_pool", bufs=2 * X_RUN))
         codes_pool = ctx.enter_context(tc.tile_pool(name="codes_pool", bufs=OUT_LAG + 3))
         result_pool = ctx.enter_context(tc.tile_pool(name="result_pool", bufs=4))
-        psum_t = ctx.enter_context(tc.psum_pool(name="psum_t", bufs=2))
-        psum_h = ctx.enter_context(tc.psum_pool(name="psum_h", bufs=4))
-        psum_o = ctx.enter_context(tc.psum_pool(name="psum_o", bufs=2))
+        psum = ctx.enter_context(tc.psum_pool(name="psum", bufs=8))
         ctx.enter_context(tc.manual_schedule())
 
         def load_x(i):
@@ -73,11 +72,11 @@ def tile_replaced_compose_lora_pa_t_kernel(tc, x, lora_A, lora_B, W, bias, lora_
         def quantise(grouped, codes, scales):
             nc.vector.quantize_mx(out=codes.bitcast(FP8X4), scales=scales, in_=grouped)
 
-        def turn_rows(rows, grouped, psum, bank_tag, leave_last_bank):
+        def turn_rows(rows, grouped, leave_last_bank):
             subs = rows.shape[1]
             grouped_words = grouped.bitcast(F32)
             for pair in range(subs // 2):
-                bank = psum.tile([P, HALVES, 2, P], F32, name="turn_bank", tag=bank_tag)
+                bank = psum.tile([P, HALVES, 2, P], F32, name="turn_bank", tag="bank")
                 for s in range(2):
                     words = rows[:, 2 * pair + s, :].bitcast(F32)
                     for u in range(HALVES):
@@ -88,12 +87,12 @@ def tile_replaced_compose_lora_pa_t_kernel(tc, x, lora_A, lora_B, W, bias, lora_
                     in_=bank[:].rearrange("p u s c -> p (s c) u"),
                 )
 
-        def weight_words(rows, psum, bank_tag, label):
+        def weight_words(rows, label):
             columns = rows.shape[1] * P
             grouped = fixed.tile([P, columns, PACK], BF16, name=label + "_grouped", align_bytes=64)
             codes = fixed.tile([P, columns], U32, name=label + "_codes", align_bytes=64)
             scales = fixed.tile([P, columns], U8, name=label + "_scales", align_bytes=64)
-            turn_rows(rows, grouped[:], psum, bank_tag, nc.vector.tensor_copy)
+            turn_rows(rows, grouped[:], nc.vector.tensor_copy)
             quantise(grouped[:].rearrange("p c t -> p (c t)"), codes[:], scales[:])
             return codes, scales
 
@@ -106,7 +105,7 @@ def tile_replaced_compose_lora_pa_t_kernel(tc, x, lora_A, lora_B, W, bias, lora_
             return b_sorted
 
         def turn_b_first(b_sorted):
-            bank = psum_o.tile([P, PACK, P], F32, name="b_bank_first", tag="out_bank")
+            bank = psum.tile([P, PACK, P], F32, name="b_bank_first", tag="bank")
             for a in range(PACK):
                 nc.tensor.transpose(out=bank[:, a, :], in_=b_sorted[:, a, :], identity=ident[:])
             b_turned = fixed.tile([P, PACK, P], F32)
@@ -117,7 +116,7 @@ def tile_replaced_compose_lora_pa_t_kernel(tc, x, lora_A, lora_B, W, bias, lora_
             return b_turned
 
         def turn_b_second(b_turned):
-            bank = psum_o.tile([P, PACK, P], F32, name="b_bank_second", tag="out_bank")
+            bank = psum.tile([P, PACK, P], F32, name="b_bank_second", tag="bank")
             for oh in range(PACK):
                 nc.tensor.transpose(out=bank[:, oh, :], in_=b_turned[:, oh, :], identity=ident[:])
             b_grouped = fixed.tile([P, d_out * PACK], BF16, align_bytes=64)
@@ -141,7 +140,7 @@ def tile_replaced_compose_lora_pa_t_kernel(tc, x, lora_A, lora_B, W, bias, lora_
             x_codes, x_scales = x_mx[i]
             for s in range(SUBS):
                 tokens = slice(s * P, (s + 1) * P)
-                bank = psum_h.tile([P, PACK, P], F32, name="h_bank", tag="h_bank")
+                bank = psum.tile([P, PACK, P], F32, name="h_bank", tag="bank")
                 for t in range(PACK):
                     ks = slice(t * P, (t + 1) * P)
                     nc.tensor.matmul_mx(
@@ -160,7 +159,7 @@ def tile_replaced_compose_lora_pa_t_kernel(tc, x, lora_A, lora_B, W, bias, lora_
             h_codes, h_scales = h_mx[i]
             out_tile = out_rows[i * TILE : (i + 1) * TILE, :].rearrange("(c s) o -> c s o", s=SUBS)
             for pair in range(SUBS // 2):
-                bank = psum_o.tile([P, 2, d_out], F32, name="out_bank", tag="out_bank")
+                bank = psum.tile([P, 2, d_out], F32, name="out_bank", tag="bank")
                 for j in range(2):
                     tokens = slice((2 * pair + j) * P, (2 * pair + j + 1) * P)
                     nc.tensor.matmul_mx(
@@ -185,39 +184,52 @@ def tile_replaced_compose_lora_pa_t_kernel(tc, x, lora_A, lora_B, W, bias, lora_
                 nc.vector.tensor_tensor(out=result[:], in0=bank[:], in1=bias_twice, op=mybir.AluOpType.add)
                 nc.sync.dma_start(out=out_tile[:, 2 * pair : 2 * pair + 2, :], in_=result[:])
 
+        grouped = {}
+
+        def open_round(r):
+            grouped[r] = grouped_pool.tile([P, 2, TILE, PACK], BF16, name="grouped", align_bytes=64)
+
+        def turn_x(tiles):
+            for i in tiles:
+                leave_last_bank = nc.vector.tensor_copy if i == tiles[-1] else nc.scalar.copy
+                turn_rows(x_in[i], grouped[i - 2][:, 1], leave_last_bank)
+
+        def quantise_round(r):
+            has_h = 0 <= r
+            has_x = r + 2 < n_tiles
+            codes = codes_pool.tile([P, 2, TILE], U32, name="codes", align_bytes=64)
+            scales = codes_pool.tile([P, 2, TILE], U8, name="scales", align_bytes=64)
+            filled = slice(0 if has_h else 1, 2 if has_x else 1)
+            quantise(
+                grouped[r][:, filled].rearrange("p g c t -> p (g c t)"),
+                codes[:, filled].rearrange("p g c -> p (g c)"),
+                scales[:, filled].rearrange("p g c -> p (g c)"),
+            )
+            h_mx[r] = (codes[:, 0], scales[:, 0])
+            x_mx[r + 2] = (codes[:, 1], scales[:, 1])
+
         def step(j):
-            has_h = 0 <= j < n_tiles
-            has_x = 0 <= j + 2 < n_tiles
-            if has_h or has_x:
-                grouped = grouped_pool.tile([P, 2, TILE, PACK], BF16, name="grouped", align_bytes=64)
-                codes = codes_pool.tile([P, 2, TILE], U32, name="codes", align_bytes=64)
-                scales = codes_pool.tile([P, 2, TILE], U8, name="scales", align_bytes=64)
-            if has_h:
-                low_rank_passes(j, grouped[:, 0])
-                h_mx[j] = (codes[:, 0], scales[:, 0])
-            if has_x:
-                by_vector = j % 2 == 0 or j < OUT_LAG
-                turn_rows(
-                    x_in[j + 2], grouped[:, 1], psum_t, "x_bank", nc.vector.tensor_copy if by_vector else nc.scalar.copy
-                )
-                x_mx[j + 2] = (codes[:, 1], scales[:, 1])
+            if j % X_RUN == 0:
+                for r in range(j, min(j + X_RUN, n_tiles)):
+                    open_round(r)
+            if j < n_tiles:
+                low_rank_passes(j, grouped[j][:, 0])
             if 0 <= j - OUT_LAG:
                 out_passes(j - OUT_LAG)
-            if has_h or has_x:
-                filled = slice(0 if has_h else 1, 2 if has_x else 1)
-                quantise(
-                    grouped[:, filled].rearrange("p g c t -> p (g c t)"),
-                    codes[:, filled].rearrange("p g c -> p (g c)"),
-                    scales[:, filled].rearrange("p g c -> p (g c)"),
-                )
+            if j % X_RUN == 0 and j + 2 < n_tiles:
+                turn_x(list(range(j + 2, j + 2 + X_RUN)))
+            if j < n_tiles:
+                quantise_round(j)
 
-        a_codes, a_scales = weight_words(a_in, psum_h, "h_bank", "a")
-        step(-2)
-        step(-1)
+        a_codes, a_scales = weight_words(a_in, "a")
+        for r in (-2, -1):
+            open_round(r)
+            turn_x([r + 2])
+            quantise_round(r)
         b_sorted = sort_b()
         step(0)
         b_turned = turn_b_first(b_sorted)
-        w_codes, w_scales = weight_words(w_in, psum_o, "out_bank", "w")
+        w_codes, w_scales = weight_words(w_in, "w")
         step(1)
         b_codes, b_scales = turn_b_second(b_turned)
         for j in range(2, n_tiles + OUT_LAG):

@@ -18,7 +18,6 @@ TILE = SUBS * P
 LORA_SCALE = 2.0
 QUARTER = 64
 OUT_LAG = 2
-X_RUN = 2
 
 FLOPS = 2 * 8192 * 512 * (512 + 256 + 256)
 
@@ -31,15 +30,17 @@ def tile_replaced_compose_lora_pa_t_kernel(tc, x, lora_A, lora_B, W, bias, lora_
     rank = lora_A.shape[1]
     d_out = W.shape[0]
     n_tiles = x_rows.shape[0] // TILE
-    assert x_rows.shape[1] == K and a_rows.shape[0] == K and d_out == 2 * P and n_tiles % X_RUN == 0
+    assert x_rows.shape[1] == K and a_rows.shape[0] == K and d_out == 2 * P
 
     with ExitStack() as ctx:
         fixed = ctx.enter_context(tc.tile_pool(name="fixed", bufs=1))
         x_pool = ctx.enter_context(tc.tile_pool(name="x_pool", bufs=n_tiles))
-        grouped_pool = ctx.enter_context(tc.tile_pool(name="grouped_pool", bufs=2 * X_RUN))
+        grouped_pool = ctx.enter_context(tc.tile_pool(name="grouped_pool", bufs=2))
         codes_pool = ctx.enter_context(tc.tile_pool(name="codes_pool", bufs=OUT_LAG + 3))
-        result_pool = ctx.enter_context(tc.tile_pool(name="result_pool", bufs=4))
-        psum = ctx.enter_context(tc.psum_pool(name="psum", bufs=8))
+        result_pool = ctx.enter_context(tc.tile_pool(name="result_pool", bufs=2 * n_tiles))
+        psum_t = ctx.enter_context(tc.psum_pool(name="psum_t", bufs=2))
+        psum_h = ctx.enter_context(tc.psum_pool(name="psum_h", bufs=4))
+        psum_o = ctx.enter_context(tc.psum_pool(name="psum_o", bufs=2))
         ctx.enter_context(tc.manual_schedule())
 
         def load_x(i):
@@ -72,11 +73,11 @@ def tile_replaced_compose_lora_pa_t_kernel(tc, x, lora_A, lora_B, W, bias, lora_
         def quantise(grouped, codes, scales):
             nc.vector.quantize_mx(out=codes.bitcast(FP8X4), scales=scales, in_=grouped)
 
-        def turn_rows(rows, grouped, leave_last_bank):
+        def turn_rows(rows, grouped, psum, bank_tag, leave_last_bank):
             subs = rows.shape[1]
             grouped_words = grouped.bitcast(F32)
             for pair in range(subs // 2):
-                bank = psum.tile([P, HALVES, 2, P], F32, name="turn_bank", tag="bank")
+                bank = psum.tile([P, HALVES, 2, P], F32, name="turn_bank", tag=bank_tag)
                 for s in range(2):
                     words = rows[:, 2 * pair + s, :].bitcast(F32)
                     for u in range(HALVES):
@@ -87,12 +88,12 @@ def tile_replaced_compose_lora_pa_t_kernel(tc, x, lora_A, lora_B, W, bias, lora_
                     in_=bank[:].rearrange("p u s c -> p (s c) u"),
                 )
 
-        def weight_words(rows, label):
+        def weight_words(rows, psum, bank_tag, label):
             columns = rows.shape[1] * P
             grouped = fixed.tile([P, columns, PACK], BF16, name=label + "_grouped", align_bytes=64)
             codes = fixed.tile([P, columns], U32, name=label + "_codes", align_bytes=64)
             scales = fixed.tile([P, columns], U8, name=label + "_scales", align_bytes=64)
-            turn_rows(rows, grouped[:], nc.vector.tensor_copy)
+            turn_rows(rows, grouped[:], psum, bank_tag, nc.vector.tensor_copy)
             quantise(grouped[:].rearrange("p c t -> p (c t)"), codes[:], scales[:])
             return codes, scales
 
@@ -105,7 +106,7 @@ def tile_replaced_compose_lora_pa_t_kernel(tc, x, lora_A, lora_B, W, bias, lora_
             return b_sorted
 
         def turn_b_first(b_sorted):
-            bank = psum.tile([P, PACK, P], F32, name="b_bank_first", tag="bank")
+            bank = psum_o.tile([P, PACK, P], F32, name="b_bank_first", tag="out_bank")
             for a in range(PACK):
                 nc.tensor.transpose(out=bank[:, a, :], in_=b_sorted[:, a, :], identity=ident[:])
             b_turned = fixed.tile([P, PACK, P], F32)
@@ -116,7 +117,7 @@ def tile_replaced_compose_lora_pa_t_kernel(tc, x, lora_A, lora_B, W, bias, lora_
             return b_turned
 
         def turn_b_second(b_turned):
-            bank = psum.tile([P, PACK, P], F32, name="b_bank_second", tag="bank")
+            bank = psum_o.tile([P, PACK, P], F32, name="b_bank_second", tag="out_bank")
             for oh in range(PACK):
                 nc.tensor.transpose(out=bank[:, oh, :], in_=b_turned[:, oh, :], identity=ident[:])
             b_grouped = fixed.tile([P, d_out * PACK], BF16, align_bytes=64)
@@ -140,7 +141,7 @@ def tile_replaced_compose_lora_pa_t_kernel(tc, x, lora_A, lora_B, W, bias, lora_
             x_codes, x_scales = x_mx[i]
             for s in range(SUBS):
                 tokens = slice(s * P, (s + 1) * P)
-                bank = psum.tile([P, PACK, P], F32, name="h_bank", tag="bank")
+                bank = psum_h.tile([P, PACK, P], F32, name="h_bank", tag="h_bank")
                 for t in range(PACK):
                     ks = slice(t * P, (t + 1) * P)
                     nc.tensor.matmul_mx(
@@ -159,7 +160,7 @@ def tile_replaced_compose_lora_pa_t_kernel(tc, x, lora_A, lora_B, W, bias, lora_
             h_codes, h_scales = h_mx[i]
             out_tile = out_rows[i * TILE : (i + 1) * TILE, :].rearrange("(c s) o -> c s o", s=SUBS)
             for pair in range(SUBS // 2):
-                bank = psum.tile([P, 2, d_out], F32, name="out_bank", tag="bank")
+                bank = psum_o.tile([P, 2, d_out], F32, name="out_bank", tag="out_bank")
                 for j in range(2):
                     tokens = slice((2 * pair + j) * P, (2 * pair + j + 1) * P)
                     nc.tensor.matmul_mx(
@@ -184,52 +185,39 @@ def tile_replaced_compose_lora_pa_t_kernel(tc, x, lora_A, lora_B, W, bias, lora_
                 nc.vector.tensor_tensor(out=result[:], in0=bank[:], in1=bias_twice, op=mybir.AluOpType.add)
                 nc.sync.dma_start(out=out_tile[:, 2 * pair : 2 * pair + 2, :], in_=result[:])
 
-        grouped = {}
-
-        def open_round(r):
-            grouped[r] = grouped_pool.tile([P, 2, TILE, PACK], BF16, name="grouped", align_bytes=64)
-
-        def turn_x(tiles):
-            for i in tiles:
-                leave_last_bank = nc.vector.tensor_copy if i == tiles[-1] else nc.scalar.copy
-                turn_rows(x_in[i], grouped[i - 2][:, 1], leave_last_bank)
-
-        def quantise_round(r):
-            has_h = 0 <= r
-            has_x = r + 2 < n_tiles
-            codes = codes_pool.tile([P, 2, TILE], U32, name="codes", align_bytes=64)
-            scales = codes_pool.tile([P, 2, TILE], U8, name="scales", align_bytes=64)
-            filled = slice(0 if has_h else 1, 2 if has_x else 1)
-            quantise(
-                grouped[r][:, filled].rearrange("p g c t -> p (g c t)"),
-                codes[:, filled].rearrange("p g c -> p (g c)"),
-                scales[:, filled].rearrange("p g c -> p (g c)"),
-            )
-            h_mx[r] = (codes[:, 0], scales[:, 0])
-            x_mx[r + 2] = (codes[:, 1], scales[:, 1])
-
         def step(j):
-            if j % X_RUN == 0:
-                for r in range(j, min(j + X_RUN, n_tiles)):
-                    open_round(r)
-            if j < n_tiles:
-                low_rank_passes(j, grouped[j][:, 0])
+            has_h = 0 <= j < n_tiles
+            has_x = 0 <= j + 2 < n_tiles
+            if has_h or has_x:
+                grouped = grouped_pool.tile([P, 2, TILE, PACK], BF16, name="grouped", align_bytes=64)
+                codes = codes_pool.tile([P, 2, TILE], U32, name="codes", align_bytes=64)
+                scales = codes_pool.tile([P, 2, TILE], U8, name="scales", align_bytes=64)
+            if has_h:
+                low_rank_passes(j, grouped[:, 0])
+                h_mx[j] = (codes[:, 0], scales[:, 0])
+            if has_x:
+                by_vector = j % 2 == 0 or j < OUT_LAG
+                turn_rows(
+                    x_in[j + 2], grouped[:, 1], psum_t, "x_bank", nc.vector.tensor_copy if by_vector else nc.scalar.copy
+                )
+                x_mx[j + 2] = (codes[:, 1], scales[:, 1])
             if 0 <= j - OUT_LAG:
                 out_passes(j - OUT_LAG)
-            if j % X_RUN == 0 and j + 2 < n_tiles:
-                turn_x(list(range(j + 2, j + 2 + X_RUN)))
-            if j < n_tiles:
-                quantise_round(j)
+            if has_h or has_x:
+                filled = slice(0 if has_h else 1, 2 if has_x else 1)
+                quantise(
+                    grouped[:, filled].rearrange("p g c t -> p (g c t)"),
+                    codes[:, filled].rearrange("p g c -> p (g c)"),
+                    scales[:, filled].rearrange("p g c -> p (g c)"),
+                )
 
-        a_codes, a_scales = weight_words(a_in, "a")
-        for r in (-2, -1):
-            open_round(r)
-            turn_x([r + 2])
-            quantise_round(r)
+        a_codes, a_scales = weight_words(a_in, psum_h, "h_bank", "a")
+        step(-2)
+        step(-1)
         b_sorted = sort_b()
         step(0)
         b_turned = turn_b_first(b_sorted)
-        w_codes, w_scales = weight_words(w_in, "w")
+        w_codes, w_scales = weight_words(w_in, psum_o, "out_bank", "w")
         step(1)
         b_codes, b_scales = turn_b_second(b_turned)
         for j in range(2, n_tiles + OUT_LAG):

from contextlib import ExitStack

import concourse.mybir as mybir
from concourse.masks import make_identity

F32 = mybir.dt.float32
BF16 = mybir.dt.bfloat16
U32 = mybir.dt.uint32
U8 = mybir.dt.uint8
FP8X4 = mybir.dt.float8_e4m3fn_x4

P = 128
PACK = 4
K = P * PACK
HALVES = 2
SUBS = 4
TILE = SUBS * P
LORA_SCALE = 2.0
QUARTER = 64
OUT_LAG = 2

FLOPS = 2 * 8192 * 512 * (512 + 256 + 256)


def tile_replaced_compose_lora_pa_t_kernel(tc, x, lora_A, lora_B, W, bias, lora_weights, out):
    nc = tc.nc
    x_rows = x.flatten_outer_dims()
    out_rows = out.flatten_outer_dims()
    a_rows = lora_A.flatten_outer_dims()
    rank = lora_A.shape[1]
    d_out = W.shape[0]
    n_tiles = x_rows.shape[0] // TILE
    assert x_rows.shape[1] == K and a_rows.shape[0] == K and d_out == 2 * P

    with ExitStack() as ctx:
        fixed = ctx.enter_context(tc.tile_pool(name="fixed", bufs=1))
        x_pool = ctx.enter_context(tc.tile_pool(name="x_pool", bufs=n_tiles))
        grouped_pool = ctx.enter_context(tc.tile_pool(name="grouped_pool", bufs=2))
        codes_pool = ctx.enter_context(tc.tile_pool(name="codes_pool", bufs=OUT_LAG + 3))
        result_pool = ctx.enter_context(tc.tile_pool(name="result_pool", bufs=2 * n_tiles))
        psum_t = ctx.enter_context(tc.psum_pool(name="psum_t", bufs=2))
        psum_h = ctx.enter_context(tc.psum_pool(name="psum_h", bufs=4))
        psum_o = ctx.enter_context(tc.psum_pool(name="psum_o", bufs=2))
        ctx.enter_context(tc.manual_schedule())

        def load_x(i):
            x_tile = x_pool.tile([P, SUBS, K], BF16, name="x_tile")
            nc.sync.dma_start(
                out=x_tile[:],
                in_=x_rows[i * TILE : (i + 1) * TILE, :].rearrange("(c s) d -> c s d", s=SUBS),
            )
            return x_tile

        a_in = fixed.tile([P, PACK, K], BF16)
        nc.sync.dma_start(out=a_in[:], in_=a_rows.rearrange("(c t) d -> c t d", t=PACK))
        x_in = [load_x(i) for i in range(2)]
        b_in = fixed.tile([P, QUARTER * rank], BF16)
        nc.sync.dma_start(out=b_in[:], in_=lora_B.rearrange("n (oh ol) r -> (n oh) (ol r)", ol=QUARTER))
        w_in = fixed.tile([P, 2, K], BF16)
        nc.sync.dma_start(out=w_in[:], in_=W.rearrange("(s c) d -> c s d", c=P))
        x_in.extend([load_x(i) for i in range(2, n_tiles)])

        mix = fixed.tile([P, 1], BF16)
        for a in range(PACK):
            nc.scalar.dma_start(out=mix[a:P:PACK, :], in_=lora_weights.rearrange("(n one) -> n one", one=1))
        bias_all = fixed.tile([P, d_out], BF16)
        nc.scalar.dma_start(out=bias_all[:], in_=bias.partition_broadcast(P))
        bias_twice = bias_all[:].unsqueeze(1).to_broadcast([P, 2, d_out])

        ident = fixed.tile([P, P], F32)
        make_identity(nc, ident[:])

        def quantise(grouped, codes, scales):
            nc.vector.quantize_mx(out=codes.bitcast(FP8X4), scales=scales, in_=grouped)

        def turn_rows(rows, grouped, psum, bank_tag, leave_last_bank):
            subs = rows.shape[1]
            grouped_words = grouped.bitcast(F32)
            for pair in range(subs // 2):
                bank = psum.tile([P, HALVES, 2, P], F32, name="turn_bank", tag=bank_tag)
                for s in range(2):
                    words = rows[:, 2 * pair + s, :].bitcast(F32)
                    for u in range(HALVES):
                        nc.tensor.transpose(out=bank[:, u, s, :], in_=words[:, u * P : (u + 1) * P], identity=ident[:])
                leave = leave_last_bank if pair == subs // 2 - 1 else nc.scalar.copy
                leave(
                    out=grouped_words[:, 2 * pair * P : 2 * (pair + 1) * P, :],
                    in_=bank[:].rearrange("p u s c -> p (s c) u"),
                )

        def weight_words(rows, psum, bank_tag, label):
            columns = rows.shape[1] * P
            grouped = fixed.tile([P, columns, PACK], BF16, name=label + "_grouped", align_bytes=64)
            codes = fixed.tile([P, columns], U32, name=label + "_codes", align_bytes=64)
            scales = fixed.tile([P, columns], U8, name=label + "_scales", align_bytes=64)
            turn_rows(rows, grouped[:], psum, bank_tag, nc.vector.tensor_copy)
            quantise(grouped[:].rearrange("p c t -> p (c t)"), codes[:], scales[:])
            return codes, scales

        def sort_b():
            b_sorted = fixed.tile([P, PACK, P], F32)
            nc.scalar.copy(
                out=b_sorted[:].rearrange("q a (ol w) -> q a ol w", w=2),
                in_=b_in[:].bitcast(F32).rearrange("q (ol a w) -> q a ol w", a=PACK, w=2),
            )
            return b_sorted

        def turn_b_first(b_sorted):
            bank = psum_o.tile([P, PACK, P], F32, name="b_bank_first", tag="out_bank")
            for a in range(PACK):
                nc.tensor.transpose(out=bank[:, a, :], in_=b_sorted[:, a, :], identity=ident[:])
            b_turned = fixed.tile([P, PACK, P], F32)
            nc.vector.tensor_copy(
                out=b_turned[:].rearrange("v oh (n a) -> v oh n a", a=PACK),
                in_=bank[:].rearrange("v a (n oh) -> v oh n a", oh=PACK),
            )
            return b_turned

        def turn_b_second(b_turned):
            bank = psum_o.tile([P, PACK, P], F32, name="b_bank_second", tag="out_bank")
            for oh in range(PACK):
                nc.tensor.transpose(out=bank[:, oh, :], in_=b_turned[:, oh, :], identity=ident[:])
            b_grouped = fixed.tile([P, d_out * PACK], BF16, align_bytes=64)
            nc.vector.tensor_scalar(
                out=b_grouped[:],
                in0=bank[:].bitcast(BF16).rearrange("q oh v -> q (oh v)"),
                scalar1=mix[:, 0:1],
                scalar2=LORA_SCALE,
                op0=mybir.AluOpType.mult,
                op1=mybir.AluOpType.mult,
            )
            codes = fixed.tile([P, d_out], U32, name="b_codes", align_bytes=64)
            scales = fixed.tile([P, d_out], U8, name="b_scales", align_bytes=64)
            quantise(b_grouped[:], codes[:], scales[:])
            return codes, scales

        x_mx = {}
        h_mx = {}

        def low_rank_passes(i, h_grouped):
            x_codes, x_scales = x_mx[i]
            for s in range(SUBS):
                tokens = slice(s * P, (s + 1) * P)
                bank = psum_h.tile([P, PACK, P], F32, name="h_bank", tag="h_bank")
                for t in range(PACK):
                    ks = slice(t * P, (t + 1) * P)
                    nc.tensor.matmul_mx(
                        out=bank[:, t, :],
                        lhsT=a_codes[:, ks].bitcast(FP8X4),
                        lhsT_scale=a_scales[:, ks],
                        rhs=x_codes[:, tokens].bitcast(FP8X4),
                        rhs_scale=x_scales[:, tokens],
                        start=True,
                        stop=True,
                    )
                nc.scalar.copy(out=h_grouped[:, tokens, :], in_=bank[:].rearrange("p t c -> p c t"))

        def out_passes(i):
            x_codes, x_scales = x_mx[i]
            h_codes, h_scales = h_mx[i]
            out_tile = out_rows[i * TILE : (i + 1) * TILE, :].rearrange("(c s) o -> c s o", s=SUBS)
            for pair in range(SUBS // 2):
                bank = psum_o.tile([P, 2, d_out], F32, name="out_bank", tag="out_bank")
                for j in range(2):
                    tokens = slice((2 * pair + j) * P, (2 * pair + j + 1) * P)
                    nc.tensor.matmul_mx(
                        out=bank[:, j, :],
                        lhsT=x_codes[:, tokens].bitcast(FP8X4),
                        lhsT_scale=x_scales[:, tokens],
                        rhs=w_codes[:].bitcast(FP8X4),
                        rhs_scale=w_scales[:],
                        start=True,
                        stop=False,
                    )
                    nc.tensor.matmul_mx(
                        out=bank[:, j, :],
                        lhsT=h_codes[:, tokens].bitcast(FP8X4),
                        lhsT_scale=h_scales[:, tokens],
                        rhs=b_codes[:].bitcast(FP8X4),
                        rhs_scale=b_scales[:],
                        start=False,
                        stop=True,
                    )
                result = result_pool.tile([P, 2, d_out], F32, name="result")
                nc.vector.tensor_tensor(out=result[:], in0=bank[:], in1=bias_twice, op=mybir.AluOpType.add)
                nc.sync.dma_start(out=out_tile[:, 2 * pair : 2 * pair + 2, :], in_=result[:])

        def step(j):
            has_h = 0 <= j < n_tiles
            has_x = 0 <= j + 2 < n_tiles
            if has_h or has_x:
                grouped = grouped_pool.tile([P, 2, TILE, PACK], BF16, name="grouped", align_bytes=64)
                codes = codes_pool.tile([P, 2, TILE], U32, name="codes", align_bytes=64)
                scales = codes_pool.tile([P, 2, TILE], U8, name="scales", align_bytes=64)
            if has_h:
                low_rank_passes(j, grouped[:, 0])
                h_mx[j] = (codes[:, 0], scales[:, 0])
            if has_x:
                by_vector = j % 2 == 0 or j < OUT_LAG
                turn_rows(
                    x_in[j + 2], grouped[:, 1], psum_t, "x_bank", nc.vector.tensor_copy if by_vector else nc.scalar.copy
                )
                x_mx[j + 2] = (codes[:, 1], scales[:, 1])
            if 0 <= j - OUT_LAG:
                out_passes(j - OUT_LAG)
            if has_h or has_x:
                filled = slice(0 if has_h else 1, 2 if has_x else 1)
                quantise(
                    grouped[:, filled].rearrange("p g c t -> p (g c t)"),
                    codes[:, filled].rearrange("p g c -> p (g c)"),
                    scales[:, filled].rearrange("p g c -> p (g c)"),
                )

        a_codes, a_scales = weight_words(a_in, psum_h, "h_bank", "a")
        step(-2)
        step(-1)
        b_sorted = sort_b()
        step(0)
        b_turned = turn_b_first(b_sorted)
        w_codes, w_scales = weight_words(w_in, psum_o, "out_bank", "w")
        step(1)
        b_codes, b_scales = turn_b_second(b_turned)
        for j in range(2, n_tiles + OUT_LAG):
            step(j)
